import numpy as np
import ml_dtypes


def mxq(x, axis, fmt="e4m3"):
    dtype, down = {"e4m3": (ml_dtypes.float8_e4m3fn, 7), "e5m2": (ml_dtypes.float8_e5m2, 14)}[fmt]
    v = np.moveaxis(np.asarray(x, np.float32).astype(ml_dtypes.bfloat16).astype(np.float64), axis, -1)
    blocks = v.reshape(v.shape[:-1] + (-1, 32))
    amax = np.abs(blocks).max(-1, keepdims=True)
    byte = np.maximum(np.where(amax > 0, np.frexp(amax)[1] - 1 + 127, 0) - down, 1)
    scale = np.exp2(byte - 127.0)
    codes = (blocks / scale).astype(np.float32).astype(dtype).astype(np.float64)
    return np.moveaxis((codes * scale).reshape(v.shape), -1, axis)


WIDE = False


def mx_kscale(k):
    if not WIDE:
        return np.ones(k)
    levels = np.array([10, -10, 5, -5, 0])
    a = np.random.permutation(np.resize(levels, k // 512 * 4)).reshape(k // 512, 4)
    idx = np.arange(k)
    return np.exp2(a[idx // 512, idx % 128 // 32])


BF16 = ml_dtypes.bfloat16


def bf(x):
    return np.asarray(x, np.float32).astype(BF16)


def f64(x):
    return np.asarray(x).astype(np.float64)


B, S, H, D = 1, 1024, 16, 128
SOFT_CAP = 20.0
BLOCKED = -30000.0


def setup_inputs():
    s = mx_kscale(S)
    query = np.random.standard_normal((B, S, H, D)) * 1.5
    key = np.random.standard_normal((B, S, H, D)) * 1.5
    value = np.random.standard_normal((B, S, H, D)) * (s.max() / s)[None, :, None, None]
    bias = np.random.standard_normal((1, 1, S, S)) * 0.5 + np.log(s)[None, None, None, :]
    bias = np.where(np.random.random((1, 1, S, S)) < 0.25, BLOCKED, bias)
    return {"query": bf(query), "key": bf(key), "value": bf(value), "attn_mask": bf(bias)}


def reference(query, key, value, attn_mask):
    q = np.swapaxes(f64(query), 1, 2)
    k = np.swapaxes(f64(key), 1, 2)
    v = np.swapaxes(f64(value), 1, 2)
    scale = q.shape[-1] ** (-0.5)
    scores = (q @ np.swapaxes(k, 2, 3)) * scale
    scores = SOFT_CAP * np.tanh(scores / SOFT_CAP)
    scores = scores + f64(attn_mask)
    e = np.exp(scores - scores.max(-1, keepdims=True))
    out = (mxq(e, 3, "e4m3") @ mxq(v, 2, "e4m3")) / e.sum(-1, keepdims=True)
    return np.swapaxes(out, 1, 2)

@@ -1,0 +1,244 @@
+import math
+from contextlib import ExitStack
+
+import concourse.mybir as mybir
+from concourse.masks import make_identity
+
+F32 = mybir.dt.float32
+BF16 = mybir.dt.bfloat16
+U32 = mybir.dt.uint32
+U8 = mybir.dt.uint8
+FP8X4 = mybir.dt.float8_e4m3fn_x4
+ACT = mybir.ActivationFunctionType
+ALU = mybir.AluOpType
+
+P = 128
+S = 1024
+H = 16
+D = 128
+NT = S // P
+NPAIR = H * NT // 2
+GH = 4
+GW = GH * D
+SOFT_CAP = 20.0
+FLOPS = 2 * 2 * H * S * S * D
+
+ADD_ON_G = True
+PINNED = True
+
+
+def s_takes_evac(k):
+    return k % 3 != 2
+
+
+def tile_naivesdpa_kernel(tc, query, key, value, attn_mask, out):
+    nc = tc.nc
+    q_v = query.rearrange("b (t p) h d -> p (b t) (h d)", p=P)
+    k_v = key.rearrange("b (t p) h d -> p (b t) (h d)", p=P)
+    v_v = value.rearrange("b (t p) h d -> p (b t) (h d)", p=P)
+    b_v = attn_mask.rearrange("a b (i p) k -> p (a b i) k", p=P)
+    o_v = out.rearrange("b (i p) h d -> p (b i) h d", p=P)
+    tanh_scale = 1.0 / (math.sqrt(D) * SOFT_CAP)
+
+    with ExitStack() as ctx:
+        sb = ctx.enter_context(tc.tile_pool(name="sb", bufs=1))
+        ps = ctx.enter_context(tc.psum_pool(name="ps", bufs=1))
+        if PINNED:
+            ctx.enter_context(tc.manual_schedule())
+
+        kraw, qraw, vraw = {}, {}, {}
+        kT, qT, vw, vs, ost = {}, {}, {}, {}, {}
+        sc, tt, uu, ww, nm, ee, rs, eT, grp, ew, es, oo = {}, {}, {}, {}, {}, {}, {}, {}, {}, {}, {}, {}
+
+        def load(store, view, g, tag):
+            r = sb.tile([P, NT, GW], BF16, name=tag, tag=tag, bufs=2)
+            nc.sync.dma_start(out=r[:], in_=view[:, :, g * GW:(g + 1) * GW])
+            store[g] = r
+
+        warm = sb.tile([P, 2], F32, name="warm", tag="warm")
+        nc.vector.memset(warm[:, 0:1], 0.0)
+        nc.scalar.activation(out=warm[:, 1:2], in_=warm[:, 0:1], func=ACT.Tanh)
+        braw = sb.tile([P, NT, S], BF16, name="braw", tag="braw")
+        b20 = sb.tile([P, NT, S], F32, name="b20", tag="b20")
+        load(kraw, k_v, 0, "kraw")
+        load(qraw, q_v, 0, "qraw")
+        nc.sync.dma_start(out=braw[:, 0:2, :], in_=b_v[:, 0:2, :])
+        load(vraw, v_v, 0, "vraw")
+        nc.sync.dma_start(out=braw[:, 2:4, :], in_=b_v[:, 2:4, :])
+        nc.sync.dma_start(out=braw[:, 4:8, :], in_=b_v[:, 4:8, :])
+        load(kraw, k_v, 1, "kraw")
+        load(qraw, q_v, 1, "qraw")
+        load(vraw, v_v, 1, "vraw")
+        ident = sb.tile([P, P], BF16, name="ident", tag="ident")
+        make_identity(nc, ident[:])
+
+        def prep_pe(raw_t, h):
+            hl = h % GH
+            pt = ps.tile([P, S], BF16, name="prep_ps", tag="tp", bufs=4)
+            for t in range(NT):
+                nc.tensor.transpose(pt[:, t * P:(t + 1) * P], raw_t[h // GH][:, t, hl * D:(hl + 1) * D], ident[:])
+            return pt
+
+        def prep_out(store, pt, h, tag, on_scalar):
+            r = sb.tile([P, S], BF16, name=tag, tag=tag, bufs=2)
+            if on_scalar:
+                nc.scalar.copy(out=r[:], in_=pt[:])
+            else:
+                nc.vector.tensor_copy(out=r[:], in_=pt[:])
+            store[h] = r
+
+        def vprep(h):
+            hl = h % GH
+            vg = sb.tile([P, S], BF16, name="vg", tag="vg", bufs=2, align_bytes=64)
+            nc.vector.tensor_copy(
+                out=vg[:].rearrange("p (g d t) -> p g d t", g=2, t=4),
+                in_=vraw[h // GH][:, :, hl * D:(hl + 1) * D].rearrange("p (g t) d -> p g d t", g=2),
+            )
+            w_ = sb.tile([P, 2 * D], U32, name="vw", tag="vw", bufs=3, align_bytes=64)
+            s_ = sb.tile([P, 2 * D], U8, name="vs", tag="vs", bufs=3, align_bytes=64)
+            nc.vector.quantize_mx(out=w_[:].bitcast(FP8X4), scales=s_[:], in_=vg[:])
+            vw[h] = w_
+            vs[h] = s_
+
+        def qk(x):
+            k, b = divmod(x, 4)
+            h = k // 4
+            i = 2 * (k % 4) + b // 2
+            c = b % 2
+            pt = ps.tile([P, 512], F32, name="sc", tag="sc", bufs=3)
+            nc.tensor.matmul(pt[:], lhsT=qT[h][:, i * P:(i + 1) * P], rhs=kT[h][:, c * 512:(c + 1) * 512], start=True, stop=True)
+            sc[x] = pt
+
+        def tanh(x):
+            k, b = divmod(x, 4)
+            nc.scalar.activation(out=tt[k][:, b // 2, (b % 2) * 512:(b % 2 + 1) * 512], in_=sc[x][:], func=ACT.Tanh, scale=tanh_scale)
+
+        def add(k):
+            ip = k % 4
+            r = sb.tile([P, 2, S], F32, name="uu", tag="uu", bufs=2)
+            eng = nc.gpsimd if ADD_ON_G else nc.vector
+            eng.tensor_tensor(out=r[:], in0=tt[k][:], in1=b20[:, 2 * ip:2 * ip + 2, :], op=ALU.add)
+            uu[k] = r
+
+        def rowmax(k, u):
+            w_ = sb.tile([P, S], F32, name="ww", tag="ww", bufs=4)
+            m_ = sb.tile([P, 1], F32, name="nm", tag="nm", bufs=6)
+            nc.vector.tensor_scalar(out=w_[:], in0=uu[k][:, u, :], scalar1=-SOFT_CAP, scalar2=None, op0=ALU.mult, op1=ALU.min, accum_out=m_[:])
+            ww[(k, u)] = w_
+            nm[(k, u)] = m_
+
+        def expo(k, u):
+            if u == 0:
+                rs[k] = sb.tile([P, 2], F32, name="rs", tag="rs", bufs=6)
+            e_ = sb.tile([P, S], BF16, name="ee", tag="ee", bufs=4)
+            nc.scalar.activation(out=e_[:], in_=ww[(k, u)][:], func=ACT.Exp, bias=nm[(k, u)][:], scale=-1.0, accum_out=rs[k][:, u:u + 1])
+            ee[(k, u)] = e_
+
+        def etrans(k, u):
+            pt = ps.tile([P, S], BF16, name="eT", tag="tp", bufs=4)
+            for j in range(NT):
+                nc.tensor.transpose(pt[:, j * P:(j + 1) * P], ee[(k, u)][:, j * P:(j + 1) * P], ident[:])
+            eT[(k, u)] = pt
+
+        def evac(k, u, on_scalar):
+            if k not in grp:
+                grp[k] = sb.tile([P, 2, S], BF16, name="grp", tag="grp", bufs=3, align_bytes=64)
+            dst = grp[k][:, u, :].rearrange("p (g q t) -> p g q t", g=2, t=4)
+            src = eT[(k, u)][:].rearrange("p (g t q) -> p g q t", g=2, t=4)
+            if on_scalar:
+                nc.scalar.copy(out=dst, in_=src)
+            else:
+                nc.vector.tensor_copy(out=dst, in_=src)
+
+        def quant(k):
+            w_ = sb.tile([P, 512], U32, name="ew", tag="ew", bufs=2, align_bytes=64)
+            s_ = sb.tile([P, 512], U8, name="es", tag="es", bufs=2, align_bytes=64)
+            nc.vector.quantize_mx(out=w_[:].bitcast(FP8X4), scales=s_[:], in_=grp[k][:].rearrange("p u c -> p (u c)"))
+            ew[k] = w_
+            es[k] = s_
+
+        def mx(k):
+            h = k // 4
+            pt = ps.tile([P, 2, D], F32, name="oo", tag="oo", bufs=1)
+            for u in range(2):
+                for g in range(2):
+                    c0 = (2 * u + g) * P
+                    nc.tensor.matmul_mx(
+                        out=pt[:, u, :],
+                        lhsT=ew[k][:, c0:c0 + P].bitcast(FP8X4),
+                        lhsT_scale=es[k][:, c0:c0 + P],
+                        rhs=vw[h][:, g * D:(g + 1) * D].bitcast(FP8X4),
+                        rhs_scale=vs[h][:, g * D:(g + 1) * D],
+                        start=(g == 0),
+                        stop=(g == 1),
+                    )
+            oo[k] = pt
+
+        def norm(k):
+            h = k // 4
+            ip = k % 4
+            if ip == 0:
+                ost[h] = sb.tile([P, NT, D], F32, name="ost", tag="ost", bufs=2)
+            rinv = sb.tile([P, 2], F32, name="rinv", tag="rinv", bufs=3)
+            nc.vector.reciprocal(rinv[:], rs[k][:])
+            nc.vector.tensor_tensor(out=ost[h][:, 2 * ip:2 * ip + 2, :], in0=oo[k][:], in1=rinv[:].unsqueeze(2).to_broadcast([P, 2, D]), op=ALU.mult)
+            if ip == 3:
+                nc.sync.dma_start(out=o_v[:, :, h, :], in_=ost[h][:])
+
+        pk = prep_pe(kraw, 0)
+        prep_out(kT, pk, 0, "kT", False)
+        pq = prep_pe(qraw, 0)
+        prep_out(qT, pq, 0, "qT", True)
+        for i in range(2):
+            nc.vector.tensor_scalar(out=b20[:, i, :], in0=braw[:, i, :], scalar1=1.0 / SOFT_CAP, scalar2=None, op0=ALU.mult)
+        vprep(0)
+        for x in range(3):
+            qk(x)
+
+        for n in range(NPAIR + 4):
+            h = n // 4
+            if n < NPAIR:
+                tt[n] = sb.tile([P, 2, S], F32, name="tt", tag="tt", bufs=2)
+                for b in range(4):
+                    tanh(4 * n + b)
+                    if 4 * n + b + 3 < 4 * NPAIR:
+                        qk(4 * n + b + 3)
+                if n < 2:
+                    for i in range(2 + 3 * n, 5 + 3 * n):
+                        nc.scalar.mul(out=b20[:, i, :], in_=braw[:, i, :], mul=1.0 / SOFT_CAP)
+                add(n)
+            pt = None
+            if h + 1 < H and n % 4 == 1:
+                pt = prep_pe(kraw, h + 1)
+            if h + 1 < H and n % 4 == 2:
+                pt = prep_pe(qraw, h + 1)
+            if 0 <= n - 2 < NPAIR:
+                rowmax(n - 2, 0)
+                rowmax(n - 2, 1)
+            if 0 <= n - 4 < NPAIR:
+                quant(n - 4)
+                mx(n - 4)
+            if h + 1 < H and n % 4 == 3:
+                vprep(h + 1)
+            if 0 <= n - 3 < NPAIR:
+                if not s_takes_evac(n - 3):
+                    evac(n - 3, 0, False)
+                evac(n - 3, 1, False)
+            if pt is not None:
+                if n % 4 == 1:
+                    prep_out(kT, pt, h + 1, "kT", False)
+                else:
+                    prep_out(qT, pt, h + 1, "qT", False)
+            if 0 <= n - 4 < NPAIR:
+                norm(n - 4)
+            if 0 <= n - 2 < NPAIR:
+                expo(n - 2, 0)
+                etrans(n - 2, 0)
+                expo(n - 2, 1)
+                etrans(n - 2, 1)
+                if s_takes_evac(n - 2):
+                    evac(n - 2, 0, True)
+            if n % 16 == 12 and n // 16 + 2 < H // GH:
+                load(kraw, k_v, n // 16 + 2, "kraw")
+                load(qraw, q_v, n // 16 + 2, "qraw")
+                load(vraw, v_v, n // 16 + 2, "vraw")

@@ -23,12 +23,11 @@ GW = GH * D
 SOFT_CAP = 20.0
 FLOPS = 2 * 2 * H * S * S * D
 
-ADD_ON_G = True
 PINNED = True
 
 
-def s_takes_evac(k):
-    return k % 3 != 2
+def s_takes_evac(k, u):
+    return u == 0 or k % 2 == 0
 
 
 def tile_naivesdpa_kernel(tc, query, key, value, attn_mask, out):
@@ -48,7 +47,7 @@ def tile_naivesdpa_kernel(tc, query, key, value, attn_mask, out):
 
         kraw, qraw, vraw = {}, {}, {}
         kT, qT, vw, vs, ost = {}, {}, {}, {}, {}
-        sc, tt, uu, ww, nm, ee, rs, eT, grp, ew, es, oo = {}, {}, {}, {}, {}, {}, {}, {}, {}, {}, {}, {}
+        sc, tt, nm, ee, rs, eT, grp, ew, es, oo = {}, {}, {}, {}, {}, {}, {}, {}, {}, {}
 
         def load(store, view, g, tag):
             r = sb.tile([P, NT, GW], BF16, name=tag, tag=tag, bufs=2)
@@ -59,7 +58,6 @@ def tile_naivesdpa_kernel(tc, query, key, value, attn_mask, out):
         nc.vector.memset(warm[:, 0:1], 0.0)
         nc.scalar.activation(out=warm[:, 1:2], in_=warm[:, 0:1], func=ACT.Tanh)
         braw = sb.tile([P, NT, S], BF16, name="braw", tag="braw")
-        b20 = sb.tile([P, NT, S], F32, name="b20", tag="b20")
         load(kraw, k_v, 0, "kraw")
         load(qraw, q_v, 0, "qraw")
         nc.sync.dma_start(out=braw[:, 0:2, :], in_=b_v[:, 0:2, :])
@@ -115,23 +113,18 @@ def tile_naivesdpa_kernel(tc, query, key, value, attn_mask, out):
 
         def add(k):
             ip = k % 4
-            r = sb.tile([P, 2, S], F32, name="uu", tag="uu", bufs=2)
-            eng = nc.gpsimd if ADD_ON_G else nc.vector
-            eng.tensor_tensor(out=r[:], in0=tt[k][:], in1=b20[:, 2 * ip:2 * ip + 2, :], op=ALU.add)
-            uu[k] = r
+            nc.vector.scalar_tensor_tensor(out=tt[k][:], in0=tt[k][:], scalar=SOFT_CAP, in1=braw[:, 2 * ip:2 * ip + 2, :], op0=ALU.mult, op1=ALU.add)
 
-        def rowmax(k, u):
-            w_ = sb.tile([P, S], F32, name="ww", tag="ww", bufs=4)
-            m_ = sb.tile([P, 1], F32, name="nm", tag="nm", bufs=6)
-            nc.vector.tensor_scalar(out=w_[:], in0=uu[k][:, u, :], scalar1=-SOFT_CAP, scalar2=None, op0=ALU.mult, op1=ALU.min, accum_out=m_[:])
-            ww[(k, u)] = w_
-            nm[(k, u)] = m_
+        def rowmax(k):
+            m_ = sb.tile([P, 2], F32, name="nm", tag="nm", bufs=4)
+            nc.vector.tensor_reduce(out=m_[:], in_=tt[k][:], axis=mybir.AxisListType.X, op=ALU.max, negate=True)
+            nm[k] = m_
 
         def expo(k, u):
             if u == 0:
                 rs[k] = sb.tile([P, 2], F32, name="rs", tag="rs", bufs=6)
             e_ = sb.tile([P, S], BF16, name="ee", tag="ee", bufs=4)
-            nc.scalar.activation(out=e_[:], in_=ww[(k, u)][:], func=ACT.Exp, bias=nm[(k, u)][:], scale=-1.0, accum_out=rs[k][:, u:u + 1])
+            nc.scalar.activation(out=e_[:], in_=tt[k][:, u, :], func=ACT.Exp, bias=nm[k][:, u:u + 1], scale=1.0, accum_out=rs[k][:, u:u + 1])
             ee[(k, u)] = e_
 
         def etrans(k, u):
@@ -189,55 +182,56 @@ def tile_naivesdpa_kernel(tc, query, key, value, attn_mask, out):
         prep_out(kT, pk, 0, "kT", False)
         pq = prep_pe(qraw, 0)
         prep_out(qT, pq, 0, "qT", True)
-        for i in range(2):
-            nc.vector.tensor_scalar(out=b20[:, i, :], in0=braw[:, i, :], scalar1=1.0 / SOFT_CAP, scalar2=None, op0=ALU.mult)
         vprep(0)
         for x in range(3):
             qk(x)
 
-        for n in range(NPAIR + 4):
+        pend = [None]
+
+        def tanh_qk(x):
+            tanh(x)
+            if x + 3 < 4 * NPAIR:
+                qk(x + 3)
+
+        for n in range(NPAIR + 5):
             h = n // 4
             if n < NPAIR:
-                tt[n] = sb.tile([P, 2, S], F32, name="tt", tag="tt", bufs=2)
-                for b in range(4):
-                    tanh(4 * n + b)
-                    if 4 * n + b + 3 < 4 * NPAIR:
-                        qk(4 * n + b + 3)
-                if n < 2:
-                    for i in range(2 + 3 * n, 5 + 3 * n):
-                        nc.scalar.mul(out=b20[:, i, :], in_=braw[:, i, :], mul=1.0 / SOFT_CAP)
-                add(n)
-            pt = None
-            if h + 1 < H and n % 4 == 1:
-                pt = prep_pe(kraw, h + 1)
-            if h + 1 < H and n % 4 == 2:
-                pt = prep_pe(qraw, h + 1)
-            if 0 <= n - 2 < NPAIR:
-                rowmax(n - 2, 0)
-                rowmax(n - 2, 1)
-            if 0 <= n - 4 < NPAIR:
-                quant(n - 4)
-                mx(n - 4)
-            if h + 1 < H and n % 4 == 3:
-                vprep(h + 1)
-            if 0 <= n - 3 < NPAIR:
-                if not s_takes_evac(n - 3):
-                    evac(n - 3, 0, False)
-                evac(n - 3, 1, False)
-            if pt is not None:
-                if n % 4 == 1:
-                    prep_out(kT, pt, h + 1, "kT", False)
-                else:
-                    prep_out(qT, pt, h + 1, "qT", False)
-            if 0 <= n - 4 < NPAIR:
-                norm(n - 4)
+                tt[n] = sb.tile([P, 2, S], F32, name="tt", tag="tt", bufs=4)
+                tanh_qk(4 * n)
+                tanh_qk(4 * n + 1)
+            if 0 <= n - 3 < NPAIR and s_takes_evac(n - 3, 1):
+                evac(n - 3, 1, True)
+            if 0 <= n - 1 < NPAIR:
+                add(n - 1)
+                rowmax(n - 1)
             if 0 <= n - 2 < NPAIR:
                 expo(n - 2, 0)
                 etrans(n - 2, 0)
+            if n < NPAIR:
+                tanh_qk(4 * n + 2)
+                tanh_qk(4 * n + 3)
+            if 0 <= n - 2 < NPAIR:
                 expo(n - 2, 1)
                 etrans(n - 2, 1)
-                if s_takes_evac(n - 2):
-                    evac(n - 2, 0, True)
+                evac(n - 2, 0, True)
+            if 0 <= n - 3 < NPAIR:
+                if not s_takes_evac(n - 3, 1):
+                    evac(n - 3, 1, False)
+                quant(n - 3)
+            if 0 <= n - 4 < NPAIR:
+                norm(n - 4)
+            if 0 <= n - 3 < NPAIR:
+                mx(n - 3)
+            if h + 1 < H and n % 4 == 1:
+                prep_out(kT, pend[0], h + 1, "kT", False)
+            if h + 1 < H and n % 4 == 2:
+                prep_out(qT, pend[0], h + 1, "qT", False)
+            if h + 1 < H and n % 4 == 0:
+                pend[0] = prep_pe(kraw, h + 1)
+            if h + 1 < H and n % 4 == 1:
+                pend[0] = prep_pe(qraw, h + 1)
+            if h + 1 < H and n % 4 == 3:
+                vprep(h + 1)
             if n % 16 == 12 and n // 16 + 2 < H // GH:
                 load(kraw, k_v, n // 16 + 2, "kraw")
                 load(qraw, q_v, n // 16 + 2, "qraw")

@@ -26,8 +26,8 @@ FLOPS = 2 * 2 * H * S * S * D
 PINNED = True
 
 
-def s_takes_evac(k, u):
-    return u == 0 or k % 2 == 0
+def s_takes_b(k):
+    return k % 4 == 0
 
 
 def tile_naivesdpa_kernel(tc, query, key, value, attn_mask, out):
@@ -47,7 +47,7 @@ def tile_naivesdpa_kernel(tc, query, key, value, attn_mask, out):
 
         kraw, qraw, vraw = {}, {}, {}
         kT, qT, vw, vs, ost = {}, {}, {}, {}, {}
-        sc, tt, nm, ee, rs, eT, grp, ew, es, oo = {}, {}, {}, {}, {}, {}, {}, {}, {}, {}
+        sc, tt, nm, ee, rs, eT, grp, ew, es, oo, ww, ri, vgs = {}, {}, {}, {}, {}, {}, {}, {}, {}, {}, {}, {}, {}
 
         def load(store, view, g, tag):
             r = sb.tile([P, NT, GW], BF16, name=tag, tag=tag, bufs=2)
@@ -85,16 +85,19 @@ def tile_naivesdpa_kernel(tc, query, key, value, attn_mask, out):
                 nc.vector.tensor_copy(out=r[:], in_=pt[:])
             store[h] = r
 
-        def vprep(h):
+        def vprep_copy(h):
             hl = h % GH
             vg = sb.tile([P, S], BF16, name="vg", tag="vg", bufs=2, align_bytes=64)
             nc.vector.tensor_copy(
                 out=vg[:].rearrange("p (g d t) -> p g d t", g=2, t=4),
                 in_=vraw[h // GH][:, :, hl * D:(hl + 1) * D].rearrange("p (g t) d -> p g d t", g=2),
             )
+            vgs[h] = vg
+
+        def vprep_quant(h):
             w_ = sb.tile([P, 2 * D], U32, name="vw", tag="vw", bufs=3, align_bytes=64)
             s_ = sb.tile([P, 2 * D], U8, name="vs", tag="vs", bufs=3, align_bytes=64)
-            nc.vector.quantize_mx(out=w_[:].bitcast(FP8X4), scales=s_[:], in_=vg[:])
+            nc.vector.quantize_mx(out=w_[:].bitcast(FP8X4), scales=s_[:], in_=vgs[h][:])
             vw[h] = w_
             vs[h] = s_
 
@@ -115,16 +118,18 @@ def tile_naivesdpa_kernel(tc, query, key, value, attn_mask, out):
             ip = k % 4
             nc.vector.scalar_tensor_tensor(out=tt[k][:], in0=tt[k][:], scalar=SOFT_CAP, in1=braw[:, 2 * ip:2 * ip + 2, :], op0=ALU.mult, op1=ALU.add)
 
-        def rowmax(k):
-            m_ = sb.tile([P, 2], F32, name="nm", tag="nm", bufs=4)
-            nc.vector.tensor_reduce(out=m_[:], in_=tt[k][:], axis=mybir.AxisListType.X, op=ALU.max, negate=True)
-            nm[k] = m_
+        def rowmax(k, u):
+            w_ = sb.tile([P, S], F32, name="ww", tag="ww", bufs=4)
+            m_ = sb.tile([P, 1], F32, name="nm", tag="nm", bufs=6)
+            nc.vector.tensor_scalar(out=w_[:], in0=tt[k][:, u, :], scalar1=-1.0, scalar2=None, op0=ALU.mult, op1=ALU.min, accum_out=m_[:])
+            ww[(k, u)] = w_
+            nm[(k, u)] = m_
 
         def expo(k, u):
             if u == 0:
-                rs[k] = sb.tile([P, 2], F32, name="rs", tag="rs", bufs=6)
+                rs[k] = sb.tile([P, 2], F32, name="rs", tag="rs", bufs=8)
             e_ = sb.tile([P, S], BF16, name="ee", tag="ee", bufs=4)
-            nc.scalar.activation(out=e_[:], in_=tt[k][:, u, :], func=ACT.Exp, bias=nm[k][:, u:u + 1], scale=1.0, accum_out=rs[k][:, u:u + 1])
+            nc.scalar.activation(out=e_[:], in_=ww[(k, u)][:], func=ACT.Exp, bias=nm[(k, u)][:], scale=-1.0, accum_out=rs[k][:, u:u + 1])
             ee[(k, u)] = e_
 
         def etrans(k, u):
@@ -167,14 +172,17 @@ def tile_naivesdpa_kernel(tc, query, key, value, attn_mask, out):
                     )
             oo[k] = pt
 
+        def recip(k):
+            r = sb.tile([P, 2], F32, name="rinv", tag="rinv", bufs=3)
+            nc.vector.reciprocal(r[:], rs[k][:])
+            ri[k] = r
+
         def norm(k):
             h = k // 4
             ip = k % 4
             if ip == 0:
                 ost[h] = sb.tile([P, NT, D], F32, name="ost", tag="ost", bufs=2)
-            rinv = sb.tile([P, 2], F32, name="rinv", tag="rinv", bufs=3)
-            nc.vector.reciprocal(rinv[:], rs[k][:])
-            nc.vector.tensor_tensor(out=ost[h][:, 2 * ip:2 * ip + 2, :], in0=oo[k][:], in1=rinv[:].unsqueeze(2).to_broadcast([P, 2, D]), op=ALU.mult)
+            nc.vector.tensor_tensor(out=ost[h][:, 2 * ip:2 * ip + 2, :], in0=oo[k][:], in1=ri[k][:].unsqueeze(2).to_broadcast([P, 2, D]), op=ALU.mult)
             if ip == 3:
                 nc.sync.dma_start(out=o_v[:, :, h, :], in_=ost[h][:])
 
@@ -182,10 +190,10 @@ def tile_naivesdpa_kernel(tc, query, key, value, attn_mask, out):
         prep_out(kT, pk, 0, "kT", False)
         pq = prep_pe(qraw, 0)
         prep_out(qT, pq, 0, "qT", True)
-        vprep(0)
+        vprep_copy(0)
         for x in range(3):
             qk(x)
-
+        vprep_quant(0)
         pend = [None]
 
         def tanh_qk(x):
@@ -193,45 +201,55 @@ def tile_naivesdpa_kernel(tc, query, key, value, attn_mask, out):
             if x + 3 < 4 * NPAIR:
                 qk(x + 3)
 
-        for n in range(NPAIR + 5):
+        def live(k):
+            return 0 <= k < NPAIR
+
+        for n in range(NPAIR + 6):
             h = n // 4
+            more = h + 1 < H
             if n < NPAIR:
-                tt[n] = sb.tile([P, 2, S], F32, name="tt", tag="tt", bufs=4)
+                tt[n] = sb.tile([P, 2, S], F32, name="tt", tag="tt", bufs=3)
                 tanh_qk(4 * n)
                 tanh_qk(4 * n + 1)
-            if 0 <= n - 3 < NPAIR and s_takes_evac(n - 3, 1):
+            if live(n - 3) and s_takes_b(n - 3):
                 evac(n - 3, 1, True)
-            if 0 <= n - 1 < NPAIR:
-                add(n - 1)
-                rowmax(n - 1)
-            if 0 <= n - 2 < NPAIR:
+            if live(n - 2):
                 expo(n - 2, 0)
                 etrans(n - 2, 0)
             if n < NPAIR:
                 tanh_qk(4 * n + 2)
                 tanh_qk(4 * n + 3)
-            if 0 <= n - 2 < NPAIR:
+            if live(n - 2):
                 expo(n - 2, 1)
                 etrans(n - 2, 1)
                 evac(n - 2, 0, True)
-            if 0 <= n - 3 < NPAIR:
-                if not s_takes_evac(n - 3, 1):
-                    evac(n - 3, 1, False)
-                quant(n - 3)
-            if 0 <= n - 4 < NPAIR:
-                norm(n - 4)
-            if 0 <= n - 3 < NPAIR:
-                mx(n - 3)
-            if h + 1 < H and n % 4 == 1:
+            if live(n - 1):
+                add(n - 1)
+            if live(n - 4):
+                quant(n - 4)
+            if live(n - 1):
+                rowmax(n - 1, 0)
+                rowmax(n - 1, 1)
+            if live(n - 5):
+                recip(n - 5)
+            if live(n - 3) and not s_takes_b(n - 3):
+                evac(n - 3, 1, False)
+            if more and n % 4 == 3:
+                vprep_copy(h + 1)
+            if live(n - 5):
+                norm(n - 5)
+            if live(n - 4):
+                mx(n - 4)
+            if more and n % 4 == 1:
                 prep_out(kT, pend[0], h + 1, "kT", False)
-            if h + 1 < H and n % 4 == 2:
+            if more and n % 4 == 2:
                 prep_out(qT, pend[0], h + 1, "qT", False)
-            if h + 1 < H and n % 4 == 0:
+            if more and n % 4 == 3:
+                vprep_quant(h + 1)
+            if more and n % 4 == 0:
                 pend[0] = prep_pe(kraw, h + 1)
-            if h + 1 < H and n % 4 == 1:
+            if more and n % 4 == 1:
                 pend[0] = prep_pe(qraw, h + 1)
-            if h + 1 < H and n % 4 == 3:
-                vprep(h + 1)
             if n % 16 == 12 and n // 16 + 2 < H // GH:
                 load(kraw, k_v, n // 16 + 2, "kraw")
                 load(qraw, q_v, n // 16 + 2, "qraw")

@@ -23,11 +23,8 @@ GW = GH * D
 SOFT_CAP = 20.0
 FLOPS = 2 * 2 * H * S * S * D
 
-PINNED = True
-
-
-def s_takes_b(k):
-    return k % 4 == 0
+V_COLS = 320
+G_COLS = S - V_COLS
 
 
 def tile_naivesdpa_kernel(tc, query, key, value, attn_mask, out):
@@ -42,12 +39,11 @@ def tile_naivesdpa_kernel(tc, query, key, value, attn_mask, out):
     with ExitStack() as ctx:
         sb = ctx.enter_context(tc.tile_pool(name="sb", bufs=1))
         ps = ctx.enter_context(tc.psum_pool(name="ps", bufs=1))
-        if PINNED:
-            ctx.enter_context(tc.manual_schedule())
+        ctx.enter_context(tc.manual_schedule())
 
         kraw, qraw, vraw = {}, {}, {}
-        kT, qT, vw, vs, ost = {}, {}, {}, {}, {}
-        sc, tt, nm, ee, rs, eT, grp, ew, es, oo, ww, ri, vgs = {}, {}, {}, {}, {}, {}, {}, {}, {}, {}, {}, {}, {}
+        kT, qT, vw, vs, ost, vgs = {}, {}, {}, {}, {}, {}
+        sc, tt, uu, nmx, nm, ee, rs, ri, eT, grp, ew, es, oo = {}, {}, {}, {}, {}, {}, {}, {}, {}, {}, {}, {}, {}
 
         def load(store, view, g, tag):
             r = sb.tile([P, NT, GW], BF16, name=tag, tag=tag, bufs=2)
@@ -58,6 +54,7 @@ def tile_naivesdpa_kernel(tc, query, key, value, attn_mask, out):
         nc.vector.memset(warm[:, 0:1], 0.0)
         nc.scalar.activation(out=warm[:, 1:2], in_=warm[:, 0:1], func=ACT.Tanh)
         braw = sb.tile([P, NT, S], BF16, name="braw", tag="braw")
+        b20 = sb.tile([P, NT, S], F32, name="b20", tag="b20")
         load(kraw, k_v, 0, "kraw")
         load(qraw, q_v, 0, "qraw")
         nc.sync.dma_start(out=braw[:, 0:2, :], in_=b_v[:, 0:2, :])
@@ -110,32 +107,40 @@ def tile_naivesdpa_kernel(tc, query, key, value, attn_mask, out):
             nc.tensor.matmul(pt[:], lhsT=qT[h][:, i * P:(i + 1) * P], rhs=kT[h][:, c * 512:(c + 1) * 512], start=True, stop=True)
             sc[x] = pt
 
-        def tanh(x):
+        def tanh_qk(x):
             k, b = divmod(x, 4)
             nc.scalar.activation(out=tt[k][:, b // 2, (b % 2) * 512:(b % 2 + 1) * 512], in_=sc[x][:], func=ACT.Tanh, scale=tanh_scale)
+            if x + 3 < 4 * NPAIR:
+                qk(x + 3)
 
-        def add(k):
+        def add_v(k):
             ip = k % 4
-            nc.vector.scalar_tensor_tensor(out=tt[k][:], in0=tt[k][:], scalar=SOFT_CAP, in1=braw[:, 2 * ip:2 * ip + 2, :], op0=ALU.mult, op1=ALU.add)
+            uu[k] = sb.tile([P, 2, S], F32, name="uu", tag="uu", bufs=4)
+            nc.vector.tensor_tensor(out=uu[k][:, :, G_COLS:], in0=tt[k][:, :, G_COLS:], in1=b20[:, 2 * ip:2 * ip + 2, G_COLS:], op=ALU.add)
 
-        def rowmax(k, u):
-            w_ = sb.tile([P, S], F32, name="ww", tag="ww", bufs=4)
-            m_ = sb.tile([P, 1], F32, name="nm", tag="nm", bufs=6)
-            nc.vector.tensor_scalar(out=w_[:], in0=tt[k][:, u, :], scalar1=-1.0, scalar2=None, op0=ALU.mult, op1=ALU.min, accum_out=m_[:])
-            ww[(k, u)] = w_
-            nm[(k, u)] = m_
+        def add_g(k):
+            ip = k % 4
+            nc.gpsimd.tensor_tensor(out=uu[k][:, :, :G_COLS], in0=tt[k][:, :, :G_COLS], in1=b20[:, 2 * ip:2 * ip + 2, :G_COLS], op=ALU.add)
+
+        def rowmax(k):
+            m_ = sb.tile([P, 2], F32, name="nmx", tag="nmx", bufs=4)
+            nc.vector.tensor_reduce(out=m_[:], in_=uu[k][:], axis=mybir.AxisListType.X, op=ALU.max, negate=True)
+            nmx[k] = m_
+
+        def scale_max(k):
+            m_ = sb.tile([P, 2], F32, name="nm", tag="nm", bufs=4)
+            nc.gpsimd.tensor_scalar(out=m_[:], in0=nmx[k][:], scalar1=SOFT_CAP, scalar2=0.0, op0=ALU.mult, op1=ALU.add)
+            nm[k] = m_
 
         def expo(k, u):
             if u == 0:
-                rs[k] = sb.tile([P, 2], F32, name="rs", tag="rs", bufs=8)
+                rs[k] = sb.tile([P, 2], F32, name="rs", tag="rs", bufs=10)
             e_ = sb.tile([P, S], BF16, name="ee", tag="ee", bufs=4)
-            nc.scalar.activation(out=e_[:], in_=ww[(k, u)][:], func=ACT.Exp, bias=nm[(k, u)][:], scale=-1.0, accum_out=rs[k][:, u:u + 1])
+            nc.scalar.activation(out=e_[:], in_=uu[k][:, u, :], func=ACT.Exp, bias=nm[k][:, u:u + 1], scale=SOFT_CAP, accum_out=rs[k][:, u:u + 1])
             ee[(k, u)] = e_
-
-        def etrans(k, u):
             pt = ps.tile([P, S], BF16, name="eT", tag="tp", bufs=4)
             for j in range(NT):
-                nc.tensor.transpose(pt[:, j * P:(j + 1) * P], ee[(k, u)][:, j * P:(j + 1) * P], ident[:])
+                nc.tensor.transpose(pt[:, j * P:(j + 1) * P], e_[:, j * P:(j + 1) * P], ident[:])
             eT[(k, u)] = pt
 
         def evac(k, u, on_scalar):
@@ -186,66 +191,66 @@ def tile_naivesdpa_kernel(tc, query, key, value, attn_mask, out):
             if ip == 3:
                 nc.sync.dma_start(out=o_v[:, :, h, :], in_=ost[h][:])
 
+        def live(k):
+            return 0 <= k < NPAIR
+
         pk = prep_pe(kraw, 0)
         prep_out(kT, pk, 0, "kT", False)
         pq = prep_pe(qraw, 0)
         prep_out(qT, pq, 0, "qT", True)
+        for i in range(2):
+            nc.vector.tensor_scalar(out=b20[:, i, :], in0=braw[:, i, :], scalar1=1.0 / SOFT_CAP, scalar2=None, op0=ALU.mult)
         vprep_copy(0)
         for x in range(3):
             qk(x)
         vprep_quant(0)
         pend = [None]
 
-        def tanh_qk(x):
-            tanh(x)
-            if x + 3 < 4 * NPAIR:
-                qk(x + 3)
-
-        def live(k):
-            return 0 <= k < NPAIR
-
-        for n in range(NPAIR + 6):
+        for n in range(NPAIR + 9):
             h = n // 4
             more = h + 1 < H
+            c = n - 2
             if n < NPAIR:
                 tt[n] = sb.tile([P, 2, S], F32, name="tt", tag="tt", bufs=3)
                 tanh_qk(4 * n)
                 tanh_qk(4 * n + 1)
-            if live(n - 3) and s_takes_b(n - 3):
-                evac(n - 3, 1, True)
-            if live(n - 2):
-                expo(n - 2, 0)
-                etrans(n - 2, 0)
+            if live(n - 3):
+                expo(n - 3, 0)
             if n < NPAIR:
                 tanh_qk(4 * n + 2)
                 tanh_qk(4 * n + 3)
-            if live(n - 2):
-                expo(n - 2, 1)
-                etrans(n - 2, 1)
-                evac(n - 2, 0, True)
-            if live(n - 1):
-                add(n - 1)
-            if live(n - 4):
-                quant(n - 4)
-            if live(n - 1):
-                rowmax(n - 1, 0)
-                rowmax(n - 1, 1)
-            if live(n - 5):
-                recip(n - 5)
-            if live(n - 3) and not s_takes_b(n - 3):
-                evac(n - 3, 1, False)
-            if more and n % 4 == 3:
+                if n < 2:
+                    for i in range(2 + 3 * n, 5 + 3 * n):
+                        nc.scalar.mul(out=b20[:, i, :], in_=braw[:, i, :], mul=1.0 / SOFT_CAP)
+            if live(n - 3):
+                expo(n - 3, 1)
+                evac(n - 3, 0, True)
+            if live(c):
+                rowmax(c)
+            if live(c - 3):
+                quant(c - 3)
+            if live(c - 4):
+                recip(c - 4)
+            if live(c + 2):
+                add_v(c + 2)
+            if more and n % 4 == 2:
                 vprep_copy(h + 1)
-            if live(n - 5):
-                norm(n - 5)
-            if live(n - 4):
-                mx(n - 4)
+            if more and n % 4 == 3:
+                vprep_quant(h + 1)
+            if live(c):
+                scale_max(c)
+            if live(c + 2):
+                add_g(c + 2)
+            if live(c - 4):
+                norm(c - 4)
+            if live(c - 3):
+                mx(c - 3)
+            if live(c - 2):
+                evac(c - 2, 1, False)
             if more and n % 4 == 1:
                 prep_out(kT, pend[0], h + 1, "kT", False)
             if more and n % 4 == 2:
                 prep_out(qT, pend[0], h + 1, "qT", False)
-            if more and n % 4 == 3:
-                vprep_quant(h + 1)
             if more and n % 4 == 0:
                 pend[0] = prep_pe(kraw, h + 1)
             if more and n % 4 == 1:

@@ -17,23 +17,57 @@ S = 1024
 H = 16
 D = 128
 NT = S // P
-NPAIR = H * NT // 2
-GH = 4
-GW = GH * D
+BANK = 512
+PACK = 4
+PASSES = S // (P * PACK)
+PAIRS_PER_HEAD = NT // 2
+NPAIR = H * PAIRS_PER_HEAD
+NBANK = 4 * NPAIR
 SOFT_CAP = 20.0
 FLOPS = 2 * 2 * H * S * S * D
 
 V_COLS = 320
 G_COLS = S - V_COLS
 
+MAX_LAG = 2
+EXP_LAG = 3
+COPY_LAG = 4
+QUANT_LAG = 5
+NORM_LAG = 6
+
+SBUF_DEPTH = {
+    "k_raw": 3,
+    "q_raw": 3,
+    "v_raw": 3,
+    "k_t": 2,
+    "q_t": 2,
+    "v_grouped": 2,
+    "v_words": 3,
+    "v_scales": 3,
+    "tanh_sb": 3,
+    "capped": EXP_LAG + 1,
+    "neg_max": 2,
+    "exp_bias": 2,
+    "e": 4,
+    "e_grouped": QUANT_LAG - EXP_LAG + 1,
+    "e_words": 2,
+    "e_scales": 2,
+    "row_sum": NORM_LAG - EXP_LAG + 1,
+    "row_inv": 2,
+    "out_sb": 2,
+}
+SCORE_BANKS = 3
+TRANSPOSE_BANKS = 4
+OUT_BANKS = 1
+
 
 def tile_naivesdpa_kernel(tc, query, key, value, attn_mask, out):
     nc = tc.nc
-    q_v = query.rearrange("b (t p) h d -> p (b t) (h d)", p=P)
-    k_v = key.rearrange("b (t p) h d -> p (b t) (h d)", p=P)
-    v_v = value.rearrange("b (t p) h d -> p (b t) (h d)", p=P)
-    b_v = attn_mask.rearrange("a b (i p) k -> p (a b i) k", p=P)
-    o_v = out.rearrange("b (i p) h d -> p (b i) h d", p=P)
+    q_rows = query.rearrange("b (j p) h d -> p (b j) h d", p=P)
+    k_rows = key.rearrange("b (j p) h d -> p (b j) h d", p=P)
+    v_rows = value.rearrange("b (j p) h d -> p (b j) h d", p=P)
+    bias_rows = attn_mask.rearrange("a b (j p) k -> p (a b j) k", p=P)
+    out_rows = out.rearrange("b (j p) h d -> p (b j) h d", p=P)
     tanh_scale = 1.0 / (math.sqrt(D) * SOFT_CAP)
 
     with ExitStack() as ctx:
@@ -41,221 +75,239 @@ def tile_naivesdpa_kernel(tc, query, key, value, attn_mask, out):
         ps = ctx.enter_context(tc.psum_pool(name="ps", bufs=1))
         ctx.enter_context(tc.manual_schedule())
 
-        kraw, qraw, vraw = {}, {}, {}
-        kT, qT, vw, vs, ost, vgs = {}, {}, {}, {}, {}, {}
-        sc, tt, uu, nmx, nm, ee, rs, ri, eT, grp, ew, es, oo = {}, {}, {}, {}, {}, {}, {}, {}, {}, {}, {}, {}, {}
+        k_raw, q_raw, v_raw, k_t, q_t, v_grouped, v_words, v_scales, out_sb = {}, {}, {}, {}, {}, {}, {}, {}, {}
+        scores, tanh_sb, capped, neg_max, exp_bias, e_t, e_grouped, e_words, e_scales = {}, {}, {}, {}, {}, {}, {}, {}, {}
+        row_sum, row_inv, out_ps = {}, {}, {}
 
-        def load(store, view, g, tag):
-            r = sb.tile([P, NT, GW], BF16, name=tag, tag=tag, bufs=2)
-            nc.sync.dma_start(out=r[:], in_=view[:, :, g * GW:(g + 1) * GW])
-            store[g] = r
+        def sbuf(tag, shape, dtype):
+            return sb.tile(shape, dtype, name=tag, tag=tag, bufs=SBUF_DEPTH[tag], align_bytes=64)
+
+        def load_head(store, rows, h, tag):
+            store[h] = sbuf(tag, [P, NT, D], BF16)
+            nc.sync.dma_start(out=store[h][:], in_=rows[:, :, h, :])
+
+        def transpose_head(raw):
+            bank = ps.tile([P, S], BF16, name="head_t", tag="t", bufs=TRANSPOSE_BANKS)
+            for j in range(NT):
+                nc.tensor.transpose(bank[:, j * P:(j + 1) * P], raw[:, j, :], ident[:])
+            return bank
+
+        def keep_head(store, bank, h, tag, copy):
+            store[h] = sbuf(tag, [P, S], BF16)
+            copy(out=store[h][:], in_=bank[:])
+
+        def group_v(h):
+            v_grouped[h] = sbuf("v_grouped", [P, S], BF16)
+            nc.vector.tensor_copy(
+                out=v_grouped[h][:].rearrange("p (g d t) -> p g d t", g=PASSES, t=PACK),
+                in_=v_raw[h][:].rearrange("p (g t) d -> p g d t", g=PASSES),
+            )
+
+        def quantise_v(h):
+            v_words[h] = sbuf("v_words", [P, PASSES * D], U32)
+            v_scales[h] = sbuf("v_scales", [P, PASSES * D], U8)
+            nc.vector.quantize_mx(out=v_words[h][:].bitcast(FP8X4), scales=v_scales[h][:], in_=v_grouped[h][:])
+
+        def scale_bias(j, mul):
+            mul(b20[:, j, :], bias_raw[:, j, :], 1.0 / SOFT_CAP)
+
+        def score_bank(x):
+            pair, b = divmod(x, 4)
+            h = pair // PAIRS_PER_HEAD
+            tile_no = 2 * (pair % PAIRS_PER_HEAD) + b // 2
+            half = b % 2
+            scores[x] = ps.tile([P, BANK], F32, name="scores", tag="scores", bufs=SCORE_BANKS)
+            nc.tensor.matmul(
+                scores[x][:],
+                lhsT=q_t[h][:, tile_no * P:(tile_no + 1) * P],
+                rhs=k_t[h][:, half * BANK:(half + 1) * BANK],
+                start=True,
+                stop=True,
+            )
+
+        def tanh_bank(x):
+            pair, b = divmod(x, 4)
+            half = b % 2
+            nc.scalar.activation(
+                out=tanh_sb[pair][:, b // 2, half * BANK:(half + 1) * BANK], in_=scores[x][:], func=ACT.Tanh, scale=tanh_scale
+            )
+            if x + SCORE_BANKS < NBANK:
+                score_bank(x + SCORE_BANKS)
+
+        def add_bias(pair, engine, cols):
+            j = 2 * (pair % PAIRS_PER_HEAD)
+            engine.tensor_tensor(
+                out=capped[pair][:, :, cols], in0=tanh_sb[pair][:, :, cols], in1=b20[:, j:j + 2, cols], op=ALU.add
+            )
+
+        def row_max(pair):
+            neg_max[pair] = sbuf("neg_max", [P, 2], F32)
+            nc.vector.tensor_reduce(
+                out=neg_max[pair][:], in_=capped[pair][:], axis=mybir.AxisListType.X, op=ALU.max, negate=True
+            )
+
+        def scale_max(pair):
+            exp_bias[pair] = sbuf("exp_bias", [P, 2], F32)
+            nc.gpsimd.tensor_scalar(
+                out=exp_bias[pair][:], in0=neg_max[pair][:], scalar1=SOFT_CAP, scalar2=0.0, op0=ALU.mult, op1=ALU.add
+            )
+
+        def exp_unit(pair, u):
+            if u == 0:
+                row_sum[pair] = sbuf("row_sum", [P, 2], F32)
+            e = sbuf("e", [P, S], BF16)
+            nc.scalar.activation(
+                out=e[:],
+                in_=capped[pair][:, u, :],
+                func=ACT.Exp,
+                bias=exp_bias[pair][:, u:u + 1],
+                scale=SOFT_CAP,
+                accum_out=row_sum[pair][:, u:u + 1],
+            )
+            e_t[(pair, u)] = ps.tile([P, S], BF16, name="e_t", tag="t", bufs=TRANSPOSE_BANKS)
+            for j in range(NT):
+                nc.tensor.transpose(e_t[(pair, u)][:, j * P:(j + 1) * P], e[:, j * P:(j + 1) * P], ident[:])
+
+        def group_e(pair, u, copy):
+            if u == 0:
+                e_grouped[pair] = sbuf("e_grouped", [P, 2, S], BF16)
+            copy(
+                out=e_grouped[pair][:, u, :].rearrange("p (g q t) -> p g q t", g=PASSES, t=PACK),
+                in_=e_t[(pair, u)][:].rearrange("p (g t q) -> p g q t", g=PASSES, t=PACK),
+            )
+
+        def quantise_e(pair):
+            e_words[pair] = sbuf("e_words", [P, 2 * PASSES * P], U32)
+            e_scales[pair] = sbuf("e_scales", [P, 2 * PASSES * P], U8)
+            nc.vector.quantize_mx(
+                out=e_words[pair][:].bitcast(FP8X4),
+                scales=e_scales[pair][:],
+                in_=e_grouped[pair][:].rearrange("p u c -> p (u c)"),
+            )
+
+        def e_times_v(pair):
+            h = pair // PAIRS_PER_HEAD
+            out_ps[pair] = ps.tile([P, 2, D], F32, name="out_ps", tag="out_ps", bufs=OUT_BANKS)
+            for u in range(2):
+                for g in range(PASSES):
+                    q_cols = slice((PASSES * u + g) * P, (PASSES * u + g + 1) * P)
+                    d_cols = slice(g * D, (g + 1) * D)
+                    nc.tensor.matmul_mx(
+                        out=out_ps[pair][:, u, :],
+                        lhsT=e_words[pair][:, q_cols].bitcast(FP8X4),
+                        lhsT_scale=e_scales[pair][:, q_cols],
+                        rhs=v_words[h][:, d_cols].bitcast(FP8X4),
+                        rhs_scale=v_scales[h][:, d_cols],
+                        start=(g == 0),
+                        stop=(g == PASSES - 1),
+                    )
+
+        def invert_sum(pair):
+            row_inv[pair] = sbuf("row_inv", [P, 2], F32)
+            nc.vector.reciprocal(row_inv[pair][:], row_sum[pair][:])
+
+        def divide_and_store(pair):
+            h, part = divmod(pair, PAIRS_PER_HEAD)
+            if part == 0:
+                out_sb[h] = sbuf("out_sb", [P, NT, D], F32)
+            nc.vector.tensor_tensor(
+                out=out_sb[h][:, 2 * part:2 * part + 2, :],
+                in0=out_ps[pair][:],
+                in1=row_inv[pair][:].unsqueeze(2).to_broadcast([P, 2, D]),
+                op=ALU.mult,
+            )
+            if part == PAIRS_PER_HEAD - 1:
+                nc.sync.dma_start(out=out_rows[:, :, h, :], in_=out_sb[h][:])
+
+        def live(pair):
+            return 0 <= pair < NPAIR
 
         warm = sb.tile([P, 2], F32, name="warm", tag="warm")
         nc.vector.memset(warm[:, 0:1], 0.0)
         nc.scalar.activation(out=warm[:, 1:2], in_=warm[:, 0:1], func=ACT.Tanh)
-        braw = sb.tile([P, NT, S], BF16, name="braw", tag="braw")
+        bias_raw = sb.tile([P, NT, S], BF16, name="bias_raw", tag="bias_raw")
         b20 = sb.tile([P, NT, S], F32, name="b20", tag="b20")
-        load(kraw, k_v, 0, "kraw")
-        load(qraw, q_v, 0, "qraw")
-        nc.sync.dma_start(out=braw[:, 0:2, :], in_=b_v[:, 0:2, :])
-        load(vraw, v_v, 0, "vraw")
-        nc.sync.dma_start(out=braw[:, 2:4, :], in_=b_v[:, 2:4, :])
-        nc.sync.dma_start(out=braw[:, 4:8, :], in_=b_v[:, 4:8, :])
-        load(kraw, k_v, 1, "kraw")
-        load(qraw, q_v, 1, "qraw")
-        load(vraw, v_v, 1, "vraw")
+        load_head(k_raw, k_rows, 0, "k_raw")
+        load_head(q_raw, q_rows, 0, "q_raw")
+        nc.sync.dma_start(out=bias_raw[:, 0:2, :], in_=bias_rows[:, 0:2, :])
+        nc.sync.dma_start(out=bias_raw[:, 2:4, :], in_=bias_rows[:, 2:4, :])
+        load_head(k_raw, k_rows, 1, "k_raw")
+        load_head(q_raw, q_rows, 1, "q_raw")
+        nc.sync.dma_start(out=bias_raw[:, 4:8, :], in_=bias_rows[:, 4:8, :])
+        load_head(v_raw, v_rows, 0, "v_raw")
+        load_head(v_raw, v_rows, 1, "v_raw")
         ident = sb.tile([P, P], BF16, name="ident", tag="ident")
         make_identity(nc, ident[:])
+        keep_head(k_t, transpose_head(k_raw[0]), 0, "k_t", nc.vector.tensor_copy)
+        keep_head(q_t, transpose_head(q_raw[0]), 0, "q_t", nc.scalar.copy)
+        scale_bias(0, nc.vector.tensor_scalar_mul)
+        scale_bias(1, nc.vector.tensor_scalar_mul)
+        for x in range(SCORE_BANKS):
+            score_bank(x)
+        waiting = {}
 
-        def prep_pe(raw_t, h):
-            hl = h % GH
-            pt = ps.tile([P, S], BF16, name="prep_ps", tag="tp", bufs=4)
-            for t in range(NT):
-                nc.tensor.transpose(pt[:, t * P:(t + 1) * P], raw_t[h // GH][:, t, hl * D:(hl + 1) * D], ident[:])
-            return pt
+        for n in range(NPAIR + NORM_LAG + 1):
+            h, part = divmod(n, PAIRS_PER_HEAD)
+            next_head = h + 1 if h + 1 < H else None
 
-        def prep_out(store, pt, h, tag, on_scalar):
-            r = sb.tile([P, S], BF16, name=tag, tag=tag, bufs=2)
-            if on_scalar:
-                nc.scalar.copy(out=r[:], in_=pt[:])
-            else:
-                nc.vector.tensor_copy(out=r[:], in_=pt[:])
-            store[h] = r
+            if live(n):
+                tanh_sb[n] = sbuf("tanh_sb", [P, 2, S], F32)
+                tanh_bank(4 * n)
+                tanh_bank(4 * n + 1)
+            if live(n - EXP_LAG):
+                exp_unit(n - EXP_LAG, 0)
+            if live(n):
+                tanh_bank(4 * n + 2)
+                tanh_bank(4 * n + 3)
+            if 1 <= n < PAIRS_PER_HEAD:
+                scale_bias(2 * n, nc.scalar.mul)
+                scale_bias(2 * n + 1, nc.scalar.mul)
+            if live(n - EXP_LAG):
+                exp_unit(n - EXP_LAG, 1)
+                group_e(n - EXP_LAG, 0, nc.scalar.copy)
 
-        def vprep_copy(h):
-            hl = h % GH
-            vg = sb.tile([P, S], BF16, name="vg", tag="vg", bufs=2, align_bytes=64)
-            nc.vector.tensor_copy(
-                out=vg[:].rearrange("p (g d t) -> p g d t", g=2, t=4),
-                in_=vraw[h // GH][:, :, hl * D:(hl + 1) * D].rearrange("p (g t) d -> p g d t", g=2),
-            )
-            vgs[h] = vg
+            if live(n - MAX_LAG):
+                row_max(n - MAX_LAG)
+            if live(n - QUANT_LAG):
+                quantise_e(n - QUANT_LAG)
+            if live(n - NORM_LAG):
+                invert_sum(n - NORM_LAG)
+            if live(n):
+                capped[n] = sbuf("capped", [P, 2, S], F32)
+                add_bias(n, nc.vector, slice(G_COLS, S))
+            if part == 2:
+                if h == 0:
+                    group_v(0)
+                if next_head is not None:
+                    group_v(next_head)
+            if part == 3:
+                if h == 0:
+                    quantise_v(0)
+                if next_head is not None:
+                    quantise_v(next_head)
 
-        def vprep_quant(h):
-            w_ = sb.tile([P, 2 * D], U32, name="vw", tag="vw", bufs=3, align_bytes=64)
-            s_ = sb.tile([P, 2 * D], U8, name="vs", tag="vs", bufs=3, align_bytes=64)
-            nc.vector.quantize_mx(out=w_[:].bitcast(FP8X4), scales=s_[:], in_=vgs[h][:])
-            vw[h] = w_
-            vs[h] = s_
+            if live(n - MAX_LAG):
+                scale_max(n - MAX_LAG)
+            if live(n):
+                add_bias(n, nc.gpsimd, slice(0, G_COLS))
 
-        def qk(x):
-            k, b = divmod(x, 4)
-            h = k // 4
-            i = 2 * (k % 4) + b // 2
-            c = b % 2
-            pt = ps.tile([P, 512], F32, name="sc", tag="sc", bufs=3)
-            nc.tensor.matmul(pt[:], lhsT=qT[h][:, i * P:(i + 1) * P], rhs=kT[h][:, c * 512:(c + 1) * 512], start=True, stop=True)
-            sc[x] = pt
+            if live(n - NORM_LAG):
+                divide_and_store(n - NORM_LAG)
+            if live(n - QUANT_LAG):
+                e_times_v(n - QUANT_LAG)
+            if live(n - COPY_LAG):
+                group_e(n - COPY_LAG, 1, nc.vector.tensor_copy)
 
-        def tanh_qk(x):
-            k, b = divmod(x, 4)
-            nc.scalar.activation(out=tt[k][:, b // 2, (b % 2) * 512:(b % 2 + 1) * 512], in_=sc[x][:], func=ACT.Tanh, scale=tanh_scale)
-            if x + 3 < 4 * NPAIR:
-                qk(x + 3)
-
-        def add_v(k):
-            ip = k % 4
-            uu[k] = sb.tile([P, 2, S], F32, name="uu", tag="uu", bufs=4)
-            nc.vector.tensor_tensor(out=uu[k][:, :, G_COLS:], in0=tt[k][:, :, G_COLS:], in1=b20[:, 2 * ip:2 * ip + 2, G_COLS:], op=ALU.add)
-
-        def add_g(k):
-            ip = k % 4
-            nc.gpsimd.tensor_tensor(out=uu[k][:, :, :G_COLS], in0=tt[k][:, :, :G_COLS], in1=b20[:, 2 * ip:2 * ip + 2, :G_COLS], op=ALU.add)
-
-        def rowmax(k):
-            m_ = sb.tile([P, 2], F32, name="nmx", tag="nmx", bufs=4)
-            nc.vector.tensor_reduce(out=m_[:], in_=uu[k][:], axis=mybir.AxisListType.X, op=ALU.max, negate=True)
-            nmx[k] = m_
-
-        def scale_max(k):
-            m_ = sb.tile([P, 2], F32, name="nm", tag="nm", bufs=4)
-            nc.gpsimd.tensor_scalar(out=m_[:], in0=nmx[k][:], scalar1=SOFT_CAP, scalar2=0.0, op0=ALU.mult, op1=ALU.add)
-            nm[k] = m_
-
-        def expo(k, u):
-            if u == 0:
-                rs[k] = sb.tile([P, 2], F32, name="rs", tag="rs", bufs=10)
-            e_ = sb.tile([P, S], BF16, name="ee", tag="ee", bufs=4)
-            nc.scalar.activation(out=e_[:], in_=uu[k][:, u, :], func=ACT.Exp, bias=nm[k][:, u:u + 1], scale=SOFT_CAP, accum_out=rs[k][:, u:u + 1])
-            ee[(k, u)] = e_
-            pt = ps.tile([P, S], BF16, name="eT", tag="tp", bufs=4)
-            for j in range(NT):
-                nc.tensor.transpose(pt[:, j * P:(j + 1) * P], e_[:, j * P:(j + 1) * P], ident[:])
-            eT[(k, u)] = pt
-
-        def evac(k, u, on_scalar):
-            if k not in grp:
-                grp[k] = sb.tile([P, 2, S], BF16, name="grp", tag="grp", bufs=3, align_bytes=64)
-            dst = grp[k][:, u, :].rearrange("p (g q t) -> p g q t", g=2, t=4)
-            src = eT[(k, u)][:].rearrange("p (g t q) -> p g q t", g=2, t=4)
-            if on_scalar:
-                nc.scalar.copy(out=dst, in_=src)
-            else:
-                nc.vector.tensor_copy(out=dst, in_=src)
-
-        def quant(k):
-            w_ = sb.tile([P, 512], U32, name="ew", tag="ew", bufs=2, align_bytes=64)
-            s_ = sb.tile([P, 512], U8, name="es", tag="es", bufs=2, align_bytes=64)
-            nc.vector.quantize_mx(out=w_[:].bitcast(FP8X4), scales=s_[:], in_=grp[k][:].rearrange("p u c -> p (u c)"))
-            ew[k] = w_
-            es[k] = s_
-
-        def mx(k):
-            h = k // 4
-            pt = ps.tile([P, 2, D], F32, name="oo", tag="oo", bufs=1)
-            for u in range(2):
-                for g in range(2):
-                    c0 = (2 * u + g) * P
-                    nc.tensor.matmul_mx(
-                        out=pt[:, u, :],
-                        lhsT=ew[k][:, c0:c0 + P].bitcast(FP8X4),
-                        lhsT_scale=es[k][:, c0:c0 + P],
-                        rhs=vw[h][:, g * D:(g + 1) * D].bitcast(FP8X4),
-                        rhs_scale=vs[h][:, g * D:(g + 1) * D],
-                        start=(g == 0),
-                        stop=(g == 1),
-                    )
-            oo[k] = pt
-
-        def recip(k):
-            r = sb.tile([P, 2], F32, name="rinv", tag="rinv", bufs=3)
-            nc.vector.reciprocal(r[:], rs[k][:])
-            ri[k] = r
-
-        def norm(k):
-            h = k // 4
-            ip = k % 4
-            if ip == 0:
-                ost[h] = sb.tile([P, NT, D], F32, name="ost", tag="ost", bufs=2)
-            nc.vector.tensor_tensor(out=ost[h][:, 2 * ip:2 * ip + 2, :], in0=oo[k][:], in1=ri[k][:].unsqueeze(2).to_broadcast([P, 2, D]), op=ALU.mult)
-            if ip == 3:
-                nc.sync.dma_start(out=o_v[:, :, h, :], in_=ost[h][:])
-
-        def live(k):
-            return 0 <= k < NPAIR
-
-        pk = prep_pe(kraw, 0)
-        prep_out(kT, pk, 0, "kT", False)
-        pq = prep_pe(qraw, 0)
-        prep_out(qT, pq, 0, "qT", True)
-        for i in range(2):
-            nc.vector.tensor_scalar(out=b20[:, i, :], in0=braw[:, i, :], scalar1=1.0 / SOFT_CAP, scalar2=None, op0=ALU.mult)
-        vprep_copy(0)
-        for x in range(3):
-            qk(x)
-        vprep_quant(0)
-        pend = [None]
-
-        for n in range(NPAIR + 9):
-            h = n // 4
-            more = h + 1 < H
-            c = n - 2
-            if n < NPAIR:
-                tt[n] = sb.tile([P, 2, S], F32, name="tt", tag="tt", bufs=3)
-                tanh_qk(4 * n)
-                tanh_qk(4 * n + 1)
-            if live(n - 3):
-                expo(n - 3, 0)
-            if n < NPAIR:
-                tanh_qk(4 * n + 2)
-                tanh_qk(4 * n + 3)
-                if n < 2:
-                    for i in range(2 + 3 * n, 5 + 3 * n):
-                        nc.scalar.mul(out=b20[:, i, :], in_=braw[:, i, :], mul=1.0 / SOFT_CAP)
-            if live(n - 3):
-                expo(n - 3, 1)
-                evac(n - 3, 0, True)
-            if live(c):
-                rowmax(c)
-            if live(c - 3):
-                quant(c - 3)
-            if live(c - 4):
-                recip(c - 4)
-            if live(c + 2):
-                add_v(c + 2)
-            if more and n % 4 == 2:
-                vprep_copy(h + 1)
-            if more and n % 4 == 3:
-                vprep_quant(h + 1)
-            if live(c):
-                scale_max(c)
-            if live(c + 2):
-                add_g(c + 2)
-            if live(c - 4):
-                norm(c - 4)
-            if live(c - 3):
-                mx(c - 3)
-            if live(c - 2):
-                evac(c - 2, 1, False)
-            if more and n % 4 == 1:
-                prep_out(kT, pend[0], h + 1, "kT", False)
-            if more and n % 4 == 2:
-                prep_out(qT, pend[0], h + 1, "qT", False)
-            if more and n % 4 == 0:
-                pend[0] = prep_pe(kraw, h + 1)
-            if more and n % 4 == 1:
-                pend[0] = prep_pe(qraw, h + 1)
-            if n % 16 == 12 and n // 16 + 2 < H // GH:
-                load(kraw, k_v, n // 16 + 2, "kraw")
-                load(qraw, q_v, n // 16 + 2, "qraw")
-                load(vraw, v_v, n // 16 + 2, "vraw")
+            if next_head is not None:
+                if part == 1:
+                    keep_head(k_t, waiting["k"], next_head, "k_t", nc.vector.tensor_copy)
+                if part == 2:
+                    keep_head(q_t, waiting["q"], next_head, "q_t", nc.vector.tensor_copy)
+                if part == 0:
+                    waiting["k"] = transpose_head(k_raw[next_head])
+                if part == 1:
+                    waiting["q"] = transpose_head(q_raw[next_head])
+            if part == 1 and h + 2 < H:
+                load_head(k_raw, k_rows, h + 2, "k_raw")
+                load_head(q_raw, q_rows, h + 2, "q_raw")
+                load_head(v_raw, v_rows, h + 2, "v_raw")

import math
from contextlib import ExitStack

import concourse.mybir as mybir
from concourse.masks import make_identity

F32 = mybir.dt.float32
BF16 = mybir.dt.bfloat16
U32 = mybir.dt.uint32
U8 = mybir.dt.uint8
FP8X4 = mybir.dt.float8_e4m3fn_x4
ACT = mybir.ActivationFunctionType
ALU = mybir.AluOpType

P = 128
S = 1024
H = 16
D = 128
NT = S // P
BANK = 512
PACK = 4
PASSES = S // (P * PACK)
PAIRS_PER_HEAD = NT // 2
NPAIR = H * PAIRS_PER_HEAD
NBANK = 4 * NPAIR
SOFT_CAP = 20.0
FLOPS = 2 * 2 * H * S * S * D

V_COLS = 320
G_COLS = S - V_COLS

MAX_LAG = 2
EXP_LAG = 3
COPY_LAG = 4
QUANT_LAG = 5
NORM_LAG = 6

SBUF_DEPTH = {
    "k_raw": 3,
    "q_raw": 3,
    "v_raw": 3,
    "k_t": 2,
    "q_t": 2,
    "v_grouped": 2,
    "v_words": 3,
    "v_scales": 3,
    "tanh_sb": 3,
    "capped": EXP_LAG + 1,
    "neg_max": 2,
    "exp_bias": 2,
    "e": 4,
    "e_grouped": QUANT_LAG - EXP_LAG + 1,
    "e_words": 2,
    "e_scales": 2,
    "row_sum": NORM_LAG - EXP_LAG + 1,
    "row_inv": 2,
    "out_sb": 2,
}
SCORE_BANKS = 3
TRANSPOSE_BANKS = 4
OUT_BANKS = 1


def tile_naivesdpa_kernel(tc, query, key, value, attn_mask, out):
    nc = tc.nc
    q_rows = query.rearrange("b (j p) h d -> p (b j) h d", p=P)
    k_rows = key.rearrange("b (j p) h d -> p (b j) h d", p=P)
    v_rows = value.rearrange("b (j p) h d -> p (b j) h d", p=P)
    bias_rows = attn_mask.rearrange("a b (j p) k -> p (a b j) k", p=P)
    out_rows = out.rearrange("b (j p) h d -> p (b j) h d", p=P)
    tanh_scale = 1.0 / (math.sqrt(D) * SOFT_CAP)

    with ExitStack() as ctx:
        sb = ctx.enter_context(tc.tile_pool(name="sb", bufs=1))
        ps = ctx.enter_context(tc.psum_pool(name="ps", bufs=1))
        ctx.enter_context(tc.manual_schedule())

        k_raw, q_raw, v_raw, k_t, q_t, v_grouped, v_words, v_scales, out_sb = {}, {}, {}, {}, {}, {}, {}, {}, {}
        scores, tanh_sb, capped, neg_max, exp_bias, e_t, e_grouped, e_words, e_scales = {}, {}, {}, {}, {}, {}, {}, {}, {}
        row_sum, row_inv, out_ps = {}, {}, {}

        def sbuf(tag, shape, dtype):
            return sb.tile(shape, dtype, name=tag, tag=tag, bufs=SBUF_DEPTH[tag], align_bytes=64)

        def load_head(store, rows, h, tag):
            store[h] = sbuf(tag, [P, NT, D], BF16)
            nc.sync.dma_start(out=store[h][:], in_=rows[:, :, h, :])

        def transpose_head(raw):
            bank = ps.tile([P, S], BF16, name="head_t", tag="t", bufs=TRANSPOSE_BANKS)
            for j in range(NT):
                nc.tensor.transpose(bank[:, j * P:(j + 1) * P], raw[:, j, :], ident[:])
            return bank

        def keep_head(store, bank, h, tag, copy):
            store[h] = sbuf(tag, [P, S], BF16)
            copy(out=store[h][:], in_=bank[:])

        def group_v(h):
            v_grouped[h] = sbuf("v_grouped", [P, S], BF16)
            nc.vector.tensor_copy(
                out=v_grouped[h][:].rearrange("p (g d t) -> p g d t", g=PASSES, t=PACK),
                in_=v_raw[h][:].rearrange("p (g t) d -> p g d t", g=PASSES),
            )

        def quantise_v(h):
            v_words[h] = sbuf("v_words", [P, PASSES * D], U32)
            v_scales[h] = sbuf("v_scales", [P, PASSES * D], U8)
            nc.vector.quantize_mx(out=v_words[h][:].bitcast(FP8X4), scales=v_scales[h][:], in_=v_grouped[h][:])

        def scale_bias(j, mul):
            mul(b20[:, j, :], bias_raw[:, j, :], 1.0 / SOFT_CAP)

        def score_bank(x):
            pair, b = divmod(x, 4)
            h = pair // PAIRS_PER_HEAD
            tile_no = 2 * (pair % PAIRS_PER_HEAD) + b // 2
            half = b % 2
            scores[x] = ps.tile([P, BANK], F32, name="scores", tag="scores", bufs=SCORE_BANKS)
            nc.tensor.matmul(
                scores[x][:],
                lhsT=q_t[h][:, tile_no * P:(tile_no + 1) * P],
                rhs=k_t[h][:, half * BANK:(half + 1) * BANK],
                start=True,
                stop=True,
            )

        def tanh_bank(x):
            pair, b = divmod(x, 4)
            half = b % 2
            nc.scalar.activation(
                out=tanh_sb[pair][:, b // 2, half * BANK:(half + 1) * BANK], in_=scores[x][:], func=ACT.Tanh, scale=tanh_scale
            )
            if x + SCORE_BANKS < NBANK:
                score_bank(x + SCORE_BANKS)

        def add_bias(pair, engine, cols):
            j = 2 * (pair % PAIRS_PER_HEAD)
            engine.tensor_tensor(
                out=capped[pair][:, :, cols], in0=tanh_sb[pair][:, :, cols], in1=b20[:, j:j + 2, cols], op=ALU.add
            )

        def row_max(pair):
            neg_max[pair] = sbuf("neg_max", [P, 2], F32)
            nc.vector.tensor_reduce(
                out=neg_max[pair][:], in_=capped[pair][:], axis=mybir.AxisListType.X, op=ALU.max, negate=True
            )

        def scale_max(pair):
            exp_bias[pair] = sbuf("exp_bias", [P, 2], F32)
            nc.gpsimd.tensor_scalar(
                out=exp_bias[pair][:], in0=neg_max[pair][:], scalar1=SOFT_CAP, scalar2=0.0, op0=ALU.mult, op1=ALU.add
            )

        def exp_unit(pair, u):
            if u == 0:
                row_sum[pair] = sbuf("row_sum", [P, 2], F32)
            e = sbuf("e", [P, S], BF16)
            nc.scalar.activation(
                out=e[:],
                in_=capped[pair][:, u, :],
                func=ACT.Exp,
                bias=exp_bias[pair][:, u:u + 1],
                scale=SOFT_CAP,
                accum_out=row_sum[pair][:, u:u + 1],
            )
            e_t[(pair, u)] = ps.tile([P, S], BF16, name="e_t", tag="t", bufs=TRANSPOSE_BANKS)
            for j in range(NT):
                nc.tensor.transpose(e_t[(pair, u)][:, j * P:(j + 1) * P], e[:, j * P:(j + 1) * P], ident[:])

        def group_e(pair, u, copy):
            if u == 0:
                e_grouped[pair] = sbuf("e_grouped", [P, 2, S], BF16)
            copy(
                out=e_grouped[pair][:, u, :].rearrange("p (g q t) -> p g q t", g=PASSES, t=PACK),
                in_=e_t[(pair, u)][:].rearrange("p (g t q) -> p g q t", g=PASSES, t=PACK),
            )

        def quantise_e(pair):
            e_words[pair] = sbuf("e_words", [P, 2 * PASSES * P], U32)
            e_scales[pair] = sbuf("e_scales", [P, 2 * PASSES * P], U8)
            nc.vector.quantize_mx(
                out=e_words[pair][:].bitcast(FP8X4),
                scales=e_scales[pair][:],
                in_=e_grouped[pair][:].rearrange("p u c -> p (u c)"),
            )

        def e_times_v(pair):
            h = pair // PAIRS_PER_HEAD
            out_ps[pair] = ps.tile([P, 2, D], F32, name="out_ps", tag="out_ps", bufs=OUT_BANKS)
            for u in range(2):
                for g in range(PASSES):
                    q_cols = slice((PASSES * u + g) * P, (PASSES * u + g + 1) * P)
                    d_cols = slice(g * D, (g + 1) * D)
                    nc.tensor.matmul_mx(
                        out=out_ps[pair][:, u, :],
                        lhsT=e_words[pair][:, q_cols].bitcast(FP8X4),
                        lhsT_scale=e_scales[pair][:, q_cols],
                        rhs=v_words[h][:, d_cols].bitcast(FP8X4),
                        rhs_scale=v_scales[h][:, d_cols],
                        start=(g == 0),
                        stop=(g == PASSES - 1),
                    )

        def invert_sum(pair):
            row_inv[pair] = sbuf("row_inv", [P, 2], F32)
            nc.vector.reciprocal(row_inv[pair][:], row_sum[pair][:])

        def divide_and_store(pair):
            h, part = divmod(pair, PAIRS_PER_HEAD)
            if part == 0:
                out_sb[h] = sbuf("out_sb", [P, NT, D], F32)
            nc.vector.tensor_tensor(
                out=out_sb[h][:, 2 * part:2 * part + 2, :],
                in0=out_ps[pair][:],
                in1=row_inv[pair][:].unsqueeze(2).to_broadcast([P, 2, D]),
                op=ALU.mult,
            )
            if part == PAIRS_PER_HEAD - 1:
                nc.sync.dma_start(out=out_rows[:, :, h, :], in_=out_sb[h][:])

        def live(pair):
            return 0 <= pair < NPAIR

        warm = sb.tile([P, 2], F32, name="warm", tag="warm")
        nc.vector.memset(warm[:, 0:1], 0.0)
        nc.scalar.activation(out=warm[:, 1:2], in_=warm[:, 0:1], func=ACT.Tanh)
        bias_raw = sb.tile([P, NT, S], BF16, name="bias_raw", tag="bias_raw")
        b20 = sb.tile([P, NT, S], F32, name="b20", tag="b20")
        load_head(k_raw, k_rows, 0, "k_raw")
        load_head(q_raw, q_rows, 0, "q_raw")
        nc.sync.dma_start(out=bias_raw[:, 0:2, :], in_=bias_rows[:, 0:2, :])
        nc.sync.dma_start(out=bias_raw[:, 2:4, :], in_=bias_rows[:, 2:4, :])
        load_head(k_raw, k_rows, 1, "k_raw")
        load_head(q_raw, q_rows, 1, "q_raw")
        nc.sync.dma_start(out=bias_raw[:, 4:8, :], in_=bias_rows[:, 4:8, :])
        load_head(v_raw, v_rows, 0, "v_raw")
        load_head(v_raw, v_rows, 1, "v_raw")
        ident = sb.tile([P, P], BF16, name="ident", tag="ident")
        make_identity(nc, ident[:])
        keep_head(k_t, transpose_head(k_raw[0]), 0, "k_t", nc.vector.tensor_copy)
        keep_head(q_t, transpose_head(q_raw[0]), 0, "q_t", nc.scalar.copy)
        scale_bias(0, nc.vector.tensor_scalar_mul)
        scale_bias(1, nc.vector.tensor_scalar_mul)
        for x in range(SCORE_BANKS):
            score_bank(x)
        waiting = {}

        for n in range(NPAIR + NORM_LAG + 1):
            h, part = divmod(n, PAIRS_PER_HEAD)
            next_head = h + 1 if h + 1 < H else None

            if live(n):
                tanh_sb[n] = sbuf("tanh_sb", [P, 2, S], F32)
                tanh_bank(4 * n)
                tanh_bank(4 * n + 1)
            if live(n - EXP_LAG):
                exp_unit(n - EXP_LAG, 0)
            if live(n):
                tanh_bank(4 * n + 2)
                tanh_bank(4 * n + 3)
            if 1 <= n < PAIRS_PER_HEAD:
                scale_bias(2 * n, nc.scalar.mul)
                scale_bias(2 * n + 1, nc.scalar.mul)
            if live(n - EXP_LAG):
                exp_unit(n - EXP_LAG, 1)
                group_e(n - EXP_LAG, 0, nc.scalar.copy)

            if live(n - MAX_LAG):
                row_max(n - MAX_LAG)
            if live(n - QUANT_LAG):
                quantise_e(n - QUANT_LAG)
            if live(n - NORM_LAG):
                invert_sum(n - NORM_LAG)
            if live(n):
                capped[n] = sbuf("capped", [P, 2, S], F32)
                add_bias(n, nc.vector, slice(G_COLS, S))
            if part == 2:
                if h == 0:
                    group_v(0)
                if next_head is not None:
                    group_v(next_head)
            if part == 3:
                if h == 0:
                    quantise_v(0)
                if next_head is not None:
                    quantise_v(next_head)

            if live(n - MAX_LAG):
                scale_max(n - MAX_LAG)
            if live(n):
                add_bias(n, nc.gpsimd, slice(0, G_COLS))

            if live(n - NORM_LAG):
                divide_and_store(n - NORM_LAG)
            if live(n - QUANT_LAG):
                e_times_v(n - QUANT_LAG)
            if live(n - COPY_LAG):
                group_e(n - COPY_LAG, 1, nc.vector.tensor_copy)

            if next_head is not None:
                if part == 1:
                    keep_head(k_t, waiting["k"], next_head, "k_t", nc.vector.tensor_copy)
                if part == 2:
                    keep_head(q_t, waiting["q"], next_head, "q_t", nc.vector.tensor_copy)
                if part == 0:
                    waiting["k"] = transpose_head(k_raw[next_head])
                if part == 1:
                    waiting["q"] = transpose_head(q_raw[next_head])
            if part == 1 and h + 2 < H:
                load_head(k_raw, k_rows, h + 2, "k_raw")
                load_head(q_raw, q_rows, h + 2, "q_raw")
                load_head(v_raw, v_rows, h + 2, "v_raw")
